import numpy as np
import ml_dtypes


def mxq(x, axis, fmt="e4m3"):
    dtype, down = {"e4m3": (ml_dtypes.float8_e4m3fn, 7), "e5m2": (ml_dtypes.float8_e5m2, 14)}[fmt]
    v = np.moveaxis(np.asarray(x, np.float32).astype(ml_dtypes.bfloat16).astype(np.float64), axis, -1)
    blocks = v.reshape(v.shape[:-1] + (-1, 32))
    amax = np.abs(blocks).max(-1, keepdims=True)
    byte = np.maximum(np.where(amax > 0, np.frexp(amax)[1] - 1 + 127, 0) - down, 1)
    scale = np.exp2(byte - 127.0)
    codes = (blocks / scale).astype(np.float32).astype(dtype).astype(np.float64)
    return np.moveaxis((codes * scale).reshape(v.shape), -1, axis)


WIDE = False


def mx_kscale(k):
    if not WIDE:
        return np.ones(k)
    levels = np.array([10, -10, 5, -5, 0])
    if k % 512:
        return np.exp2(np.random.permutation(np.resize(levels, k // 32))).repeat(32)
    a = np.empty((k // 512, 16))
    for p in range(k // 512):
        a[p, :8] = np.random.permutation(np.resize(levels, 8))
        for g in range(8):
            far = levels[np.abs(levels - a[p, g]) >= 10]
            a[p, g + 8] = far[np.random.randint(len(far))]
    return np.exp2(a.ravel()).repeat(32)


BF16 = ml_dtypes.bfloat16


def bf(x):
    return np.asarray(x, np.float32).astype(BF16)


def f64(x):
    return np.asarray(x).astype(np.float64)


N, E, C, D1, D2 = 1024, 2048, 512, 2, 2
T1 = D1 + 1


def shift_down(y, k):
    return np.pad(y, ((k, 0), (0, 0)))[:y.shape[0]] if k > 0 else y


def setup_inputs():
    s = mx_kscale(E)
    return {"x": bf(np.random.standard_normal((N, E)) * s),
            "W1": bf(np.random.standard_normal((T1, E, C)) * 0.4 / np.sqrt(E) / s[None, :, None]),
            "b1": bf(np.random.standard_normal((1, C)) * 0.25)}


def reference(x, W1, b1):
    Y = mxq(f64(x), 1, "e4m3") @ mxq(f64(W1), 1, "e4m3")
    S = sum(shift_down(Y[k], k) for k in range(T1))
    cnt1 = np.minimum(np.arange(N), D1) + 1.0
    return np.tanh(S + cnt1[:, None] * f64(b1)[0])

@@ -1,0 +1,252 @@
+from contextlib import ExitStack
+
+import concourse.mybir as mybir
+from concourse.masks import make_identity
+
+F32 = mybir.dt.float32
+BF16 = mybir.dt.bfloat16
+U32 = mybir.dt.uint32
+U8 = mybir.dt.uint8
+FP8X4 = mybir.dt.float8_e4m3fn_x4
+ACT = mybir.ActivationFunctionType
+ALU = mybir.AluOpType
+
+P = 128
+ROWS, K_DIM, COLS, TAPS = 1024, 2048, 512, 3
+SLAB = 4 * P
+SLABS = K_DIM // SLAB
+CHUNKS = SLABS * TAPS
+TILES = ROWS // P
+SLOTS = TILES + 2
+MOVED = 6
+
+PAIRS = (6, 0, 2)
+SINGLES = (4, 5)
+EARLY = (6, 7, 0, 1, 2, 3, 4)
+LATE = 5
+LATE_GROUPS = ((7, 0, 256), (0, 256, 384), (1, 384, 512))
+CHUNK_BY_CHUNK = 9
+VECTOR_COLS = (336, 400, 224) + (192,) * 9
+
+FLOPS = 2 * ROWS * K_DIM * COLS * TAPS
+
+
+def slot_of(j, tap):
+    source = j - tap
+    return source if source >= 0 else source + SLOTS
+
+
+def tile_predictor_pa_kernel(tc, x, W1, b1, out):
+    nc = tc.nc
+    with ExitStack() as ctx:
+        keep = ctx.enter_context(tc.tile_pool(name="keep", bufs=1))
+        stage = ctx.enter_context(tc.tile_pool(name="stage", bufs=3))
+        psum = ctx.enter_context(tc.psum_pool(name="psum", bufs=1))
+        ctx.enter_context(tc.manual_schedule())
+
+        x_rows = x.rearrange("(i j) k -> i j k", j=TILES)
+        x_sb = {}
+        w_raw = {}
+
+        def load_chunk(c):
+            g, tap = divmod(c, TAPS)
+            w_raw[c] = keep.tile([P, 4, COLS], BF16, name="w_raw%d" % c)
+            nc.sync.dma_start(
+                out=w_raw[c][:],
+                in_=W1[tap, SLAB * g : SLAB * (g + 1), :].rearrange("(q t) c -> q t c", t=4),
+            )
+
+        load_chunk(0)
+        for j in (6, 7, 0, 1, 2, 3, 4, 5):
+            x_sb[j] = keep.tile([P, K_DIM], BF16, name="x_sb%d" % j)
+            nc.sync.dma_start(out=x_sb[j][:], in_=x_rows[:, j, :])
+        for c in range(1, CHUNKS):
+            load_chunk(c)
+
+        bias_row = keep.tile([P, COLS], BF16, name="bias_row")
+        nc.vector.memset(bias_row[:], 0.0)
+        nc.scalar.dma_start(out=bias_row[0:1, :], in_=b1[0:1, :])
+        ones = keep.tile([P, P], BF16, name="ones")
+        nc.vector.memset(ones[:], 1.0)
+        table_in = keep.tile([P, 1], F32, name="table_in")
+        table_out = keep.tile([P, 1], F32, name="table_out")
+        nc.vector.memset(table_in[:], 0.0)
+        nc.scalar.activation(out=table_out[:], in_=table_in[:], func=ACT.Tanh)
+        ident = keep.tile([P, P], F32, name="ident")
+        make_identity(nc, ident[:])
+        count0 = keep.tile([P, 1], F32, name="count0")
+        count1 = keep.tile([P, 1], F32, name="count1")
+        nc.vector.memset(count0[:], 3.0)
+        nc.vector.memset(count0[0:1, :], 1.0)
+        nc.vector.memset(count1[:], 3.0)
+        nc.vector.memset(count1[0:1, :], 2.0)
+
+        xg, xg_words, xc, xs = [], [], [], []
+        for g in range(SLABS):
+            grouped = keep.tile([P, SLOTS, P, 4], BF16, name="xg%d" % g, align_bytes=64)
+            nc.vector.memset(grouped[:, TILES:SLOTS, :, :], 0.0)
+            xg.append(grouped)
+            xg_words.append(grouped[:].bitcast(F32))
+            xc.append(keep.tile([P, SLOTS, P], U32, name="xc%d" % g, align_bytes=64))
+            xs.append(keep.tile([P, SLOTS, P], U8, name="xs%d" % g, align_bytes=64))
+        wc, ws, wg = [], [], {}
+        for c in range(CHUNKS):
+            wc.append(keep.tile([P, COLS], U32, name="wc%d" % c, align_bytes=64))
+            ws.append(keep.tile([P, COLS], U8, name="ws%d" % c, align_bytes=64))
+        bias1 = keep.tile([P, COLS], F32, name="bias1")
+        bias3 = keep.tile([P, COLS], F32, name="bias3")
+        bias_tile0 = keep.tile([P, COLS], F32, name="bias_tile0")
+        bias_tile1 = keep.tile([P, COLS], F32, name="bias_tile1")
+        bias_of = {0: bias_tile0, 1: bias_tile1}
+
+        def quantise_x(g, first, end):
+            nc.vector.quantize_mx(
+                out=xc[g][:, first:end, :].rearrange("p s r -> p (s r)").bitcast(FP8X4),
+                scales=xs[g][:, first:end, :].rearrange("p s r -> p (s r)"),
+                in_=xg[g][:, first:end, :, :].rearrange("p s r t -> p (s r t)"),
+            )
+
+        def move_by_one_column(g):
+            nc.vector.tensor_copy(
+                out=xg[g][:, TILES:SLOTS, 1:P, :].rearrange("p s r t -> p s (r t)"),
+                in_=xg[g][:, MOVED : MOVED + 2, 0 : P - 1, :].rearrange("p s r t -> p s (r t)"),
+            )
+
+        def regroup(c):
+            wg[c] = stage.tile([P, COLS, 4], BF16, tag="wg", name="wg%d" % c, align_bytes=64)
+            for copy, first, end in (
+                (nc.vector.tensor_copy, 0, VECTOR_COLS[c]),
+                (nc.scalar.copy, VECTOR_COLS[c], COLS),
+            ):
+                copy(
+                    out=wg[c][:, first:end, :].rearrange("p (c i) t -> p c t i", i=4),
+                    in_=w_raw[c][:, :, first:end].rearrange("p t (c i) -> p c t i", i=4),
+                )
+
+        def quantise_chunk(c):
+            nc.vector.quantize_mx(
+                out=wc[c][:].bitcast(FP8X4),
+                scales=ws[c][:],
+                in_=wg[c][:].rearrange("p c t -> p (c t)"),
+            )
+
+        def transpose_tile(j, targets):
+            words = x_sb[j][:].bitcast(F32)
+            for g in range(SLABS):
+                for u in range(2):
+                    nc.tensor.transpose(targets[g][:, u, :], words[:, 256 * g + u : 256 * (g + 1) : 2], ident[:])
+
+        regroup(0)
+        quantise_chunk(0)
+
+        for n, j0 in enumerate(PAIRS):
+            banks = []
+            for g in range(SLABS):
+                banks.append(psum.tile([P, 2, 2, P], F32, tag="bank%d" % (4 * (n % 2) + g), name="pair%d_%d" % (j0, g)))
+            transpose_tile(j0, [bank[:, 0, :, :] for bank in banks])
+            if n == 0:
+                bias_ps = psum.tile([P, COLS], F32, tag="bank7", name="bias_ps")
+                nc.tensor.matmul(out=bias_ps[:], lhsT=ones[:], rhs=bias_row[:], start=True, stop=True)
+                nc.scalar.copy(out=bias1[:], in_=bias_ps[:])
+            transpose_tile(j0 + 1, [bank[:, 1, :, :] for bank in banks])
+
+            def copy_out_pair(copy, g):
+                copy(out=xg_words[g][:, j0 : j0 + 2, :, :], in_=banks[g][:].rearrange("p j u r -> p j r u"))
+
+            copy_out_pair(nc.scalar.copy, 0)
+            copy_out_pair(nc.vector.tensor_copy, 1)
+            copy_out_pair(nc.scalar.copy, 2)
+            quantise_x(0, j0, j0 + 2)
+            copy_out_pair(nc.scalar.copy, 3)
+            if n == 0:
+                move_by_one_column(0)
+            if n == 1:
+                quantise_x(0, TILES, SLOTS)
+            for g in range(1, SLABS if n < 2 else 2):
+                quantise_x(g, j0, j0 + 2)
+
+        halves = {}
+        for n, j in enumerate(SINGLES):
+            halves[j] = []
+            for h in range(2):
+                halves[j].append(psum.tile([P, 2, 2, P], F32, tag="bank%d" % (4 + 2 * n + h), name="single%d_%d" % (j, h)))
+
+        def copy_out_single(copy, j, g):
+            copy(out=xg_words[g][:, j, :, :], in_=halves[j][g // 2][:, g % 2, :, :].rearrange("p u r -> p r u"))
+
+        transpose_tile(4, [halves[4][g // 2][:, g % 2, :, :] for g in range(SLABS)])
+        copy_out_single(nc.scalar.copy, 4, 0)
+        copy_out_single(nc.vector.tensor_copy, 4, 1)
+        copy_out_single(nc.scalar.copy, 4, 2)
+        copy_out_single(nc.vector.tensor_copy, 4, 3)
+        quantise_x(0, 4, 5)
+        transpose_tile(5, [halves[5][g // 2][:, g % 2, :, :] for g in range(SLABS)])
+        copy_out_single(nc.scalar.copy, 5, 0)
+        copy_out_single(nc.vector.tensor_copy, 5, 1)
+
+        acc = {}
+        for bank, j in enumerate(EARLY):
+            acc[j] = psum.tile([P, COLS], F32, tag="bank%d" % bank, name="acc%d" % j)
+
+        def mx_pass(target, j, c, first, end):
+            g, tap = divmod(c, TAPS)
+            s = slot_of(j, tap)
+            nc.tensor.matmul_mx(
+                out=target,
+                lhsT=xc[g][:, s, :].bitcast(FP8X4),
+                lhsT_scale=xs[g][:, s, :],
+                rhs=wc[c][:, first:end].bitcast(FP8X4),
+                rhs_scale=ws[c][:, first:end],
+                start=(c == 0),
+                stop=(c == CHUNKS - 1),
+            )
+
+        for j in EARLY:
+            mx_pass(acc[j][:], j, 0, 0, COLS)
+        regroup(1)
+        quantise_chunk(1)
+        quantise_x(0, 5, 6)
+        for j in (7, 0, 1, 2, 3, 4, 6):
+            mx_pass(acc[j][:], j, 1, 0, COLS)
+        copy_out_single(nc.scalar.copy, 5, 2)
+        copy_out_single(nc.vector.tensor_copy, 5, 3)
+        for c in range(2, CHUNKS):
+            regroup(c)
+            g = c // 2
+            if g < SLABS:
+                if c % 2 == 0:
+                    quantise_x(g, 4, 6)
+                else:
+                    move_by_one_column(g)
+            quantise_chunk(c)
+            if g < SLABS:
+                if c % 2 == 1:
+                    quantise_x(g, TILES, SLOTS)
+                elif g >= 2:
+                    quantise_x(g, 2, 4)
+            if c < CHUNK_BY_CHUNK:
+                for j in EARLY:
+                    mx_pass(acc[j][:], j, c, 0, COLS)
+
+        nc.vector.tensor_scalar(out=bias3[:], in0=bias1[:], scalar1=3.0, scalar2=None, op0=ALU.mult)
+        nc.vector.tensor_scalar(out=bias_tile0[:], in0=bias1[:], scalar1=count0[:, 0:1], scalar2=None, op0=ALU.mult)
+        nc.vector.tensor_scalar(out=bias_tile1[:], in0=bias1[:], scalar1=count1[:, 0:1], scalar2=None, op0=ALU.mult)
+
+        out_rows = out.rearrange("(i j) c -> i j c", j=TILES)
+
+        def finish(sums, j, first, end):
+            summed = stage.tile([P, end - first], F32, tag="summed", name="summed%d_%d" % (j, first))
+            nc.vector.tensor_tensor(out=summed[:], in0=sums, in1=bias_of.get(j, bias3)[:, first:end], op=ALU.add)
+            result = keep.tile([P, end - first], F32, name="result%d_%d" % (j, first))
+            nc.scalar.activation(out=result[:], in_=summed[:], func=ACT.Tanh)
+            nc.sync.dma_start(out=out_rows[:, j, first:end], in_=result[:])
+
+        for j in EARLY:
+            for c in range(CHUNK_BY_CHUNK, CHUNKS):
+                mx_pass(acc[j][:], j, c, 0, COLS)
+            finish(acc[j][:], j, 0, COLS)
+        for bank, first, end in LATE_GROUPS:
+            late = psum.tile([P, end - first], F32, tag="bank%d" % bank, name="late%d" % first)
+            for c in range(CHUNKS):
+                mx_pass(late[:], LATE, c, first, end)
+            finish(late[:], LATE, first, end)

@@ -62,12 +62,9 @@ def tile_predictor_pa_kernel(tc, x, W1, b1, out):
             nc.sync.dma_start(out=x_sb[j][:], in_=x_rows[:, j, :])
         for c in range(1, CHUNKS):
             load_chunk(c)
+        bias = keep.tile([P, COLS], BF16, name="bias")
+        nc.sync.dma_start(out=bias[:], in_=b1.rearrange("o c -> (o c)").partition_broadcast(P))
 
-        bias_row = keep.tile([P, COLS], BF16, name="bias_row")
-        nc.vector.memset(bias_row[:], 0.0)
-        nc.scalar.dma_start(out=bias_row[0:1, :], in_=b1[0:1, :])
-        ones = keep.tile([P, P], BF16, name="ones")
-        nc.vector.memset(ones[:], 1.0)
         table_in = keep.tile([P, 1], F32, name="table_in")
         table_out = keep.tile([P, 1], F32, name="table_out")
         nc.vector.memset(table_in[:], 0.0)
@@ -80,6 +77,7 @@ def tile_predictor_pa_kernel(tc, x, W1, b1, out):
         nc.vector.memset(count0[0:1, :], 1.0)
         nc.vector.memset(count1[:], 3.0)
         nc.vector.memset(count1[0:1, :], 2.0)
+        count_of = {0: count0[:, 0:1], 1: count1[:, 0:1]}
 
         xg, xg_words, xc, xs = [], [], [], []
         for g in range(SLABS):
@@ -93,11 +91,6 @@ def tile_predictor_pa_kernel(tc, x, W1, b1, out):
         for c in range(CHUNKS):
             wc.append(keep.tile([P, COLS], U32, name="wc%d" % c, align_bytes=64))
             ws.append(keep.tile([P, COLS], U8, name="ws%d" % c, align_bytes=64))
-        bias1 = keep.tile([P, COLS], F32, name="bias1")
-        bias3 = keep.tile([P, COLS], F32, name="bias3")
-        bias_tile0 = keep.tile([P, COLS], F32, name="bias_tile0")
-        bias_tile1 = keep.tile([P, COLS], F32, name="bias_tile1")
-        bias_of = {0: bias_tile0, 1: bias_tile1}
 
         def quantise_x(g, first, end):
             nc.vector.quantize_mx(
@@ -144,10 +137,6 @@ def tile_predictor_pa_kernel(tc, x, W1, b1, out):
             for g in range(SLABS):
                 banks.append(psum.tile([P, 2, 2, P], F32, tag="bank%d" % (4 * (n % 2) + g), name="pair%d_%d" % (j0, g)))
             transpose_tile(j0, [bank[:, 0, :, :] for bank in banks])
-            if n == 0:
-                bias_ps = psum.tile([P, COLS], F32, tag="bank7", name="bias_ps")
-                nc.tensor.matmul(out=bias_ps[:], lhsT=ones[:], rhs=bias_row[:], start=True, stop=True)
-                nc.scalar.copy(out=bias1[:], in_=bias_ps[:])
             transpose_tile(j0 + 1, [bank[:, 1, :, :] for bank in banks])
 
             def copy_out_pair(copy, g):
@@ -228,15 +217,13 @@ def tile_predictor_pa_kernel(tc, x, W1, b1, out):
                 for j in EARLY:
                     mx_pass(acc[j][:], j, c, 0, COLS)
 
-        nc.vector.tensor_scalar(out=bias3[:], in0=bias1[:], scalar1=3.0, scalar2=None, op0=ALU.mult)
-        nc.vector.tensor_scalar(out=bias_tile0[:], in0=bias1[:], scalar1=count0[:, 0:1], scalar2=None, op0=ALU.mult)
-        nc.vector.tensor_scalar(out=bias_tile1[:], in0=bias1[:], scalar1=count1[:, 0:1], scalar2=None, op0=ALU.mult)
-
         out_rows = out.rearrange("(i j) c -> i j c", j=TILES)
 
         def finish(sums, j, first, end):
             summed = stage.tile([P, end - first], F32, tag="summed", name="summed%d_%d" % (j, first))
-            nc.vector.tensor_tensor(out=summed[:], in0=sums, in1=bias_of.get(j, bias3)[:, first:end], op=ALU.add)
+            nc.vector.scalar_tensor_tensor(
+                out=summed[:], in0=bias[:, first:end], scalar=count_of.get(j, 3.0), in1=sums, op0=ALU.mult, op1=ALU.add
+            )
             result = keep.tile([P, end - first], F32, name="result%d_%d" % (j, first))
             nc.scalar.activation(out=result[:], in_=summed[:], func=ACT.Tanh)
             nc.sync.dma_start(out=out_rows[:, j, first:end], in_=result[:])

@@ -56,10 +56,15 @@ def tile_predictor_pa_kernel(tc, x, W1, b1, out):
                 in_=W1[tap, SLAB * g : SLAB * (g + 1), :].rearrange("(q t) c -> q t c", t=4),
             )
 
-        load_chunk(0)
         for j in (6, 7, 0, 1, 2, 3, 4, 5):
             x_sb[j] = keep.tile([P, K_DIM], BF16, name="x_sb%d" % j)
-            nc.sync.dma_start(out=x_sb[j][:], in_=x_rows[:, j, :])
+            if j == 4:
+                load_chunk(0)
+            pieces = 2 if j == 6 else 1
+            width = K_DIM // pieces
+            for piece in range(pieces):
+                cols = slice(piece * width, (piece + 1) * width)
+                nc.sync.dma_start(out=x_sb[j][:, cols], in_=x_rows[:, j, cols])
         for c in range(1, CHUNKS):
             load_chunk(c)
         bias = keep.tile([P, COLS], BF16, name="bias")
@@ -129,9 +134,6 @@ def tile_predictor_pa_kernel(tc, x, W1, b1, out):
                 for u in range(2):
                     nc.tensor.transpose(targets[g][:, u, :], words[:, 256 * g + u : 256 * (g + 1) : 2], ident[:])
 
-        regroup(0)
-        quantise_chunk(0)
-
         for n, j0 in enumerate(PAIRS):
             banks = []
             for g in range(SLABS):
@@ -153,6 +155,9 @@ def tile_predictor_pa_kernel(tc, x, W1, b1, out):
                 quantise_x(0, TILES, SLOTS)
             for g in range(1, SLABS if n < 2 else 2):
                 quantise_x(g, j0, j0 + 2)
+
+        regroup(0)
+        quantise_chunk(0)
 
         halves = {}
         for n, j in enumerate(SINGLES):

@@ -82,7 +82,7 @@ def tile_predictor_pa_kernel(tc, x, W1, b1, out):
         nc.vector.memset(count0[0:1, :], 1.0)
         nc.vector.memset(count1[:], 3.0)
         nc.vector.memset(count1[0:1, :], 2.0)
-        count_of = {0: count0[:, 0:1], 1: count1[:, 0:1]}
+
 
         xg, xg_words, xc, xs = [], [], [], []
         for g in range(SLABS):
@@ -96,6 +96,11 @@ def tile_predictor_pa_kernel(tc, x, W1, b1, out):
         for c in range(CHUNKS):
             wc.append(keep.tile([P, COLS], U32, name="wc%d" % c, align_bytes=64))
             ws.append(keep.tile([P, COLS], U8, name="ws%d" % c, align_bytes=64))
+
+        bias3 = keep.tile([P, COLS], F32, name="bias3")
+        bias_tile0 = keep.tile([P, COLS], F32, name="bias_tile0")
+        bias_tile1 = keep.tile([P, COLS], F32, name="bias_tile1")
+        bias_of = {0: bias_tile0, 1: bias_tile1}
 
         def quantise_x(g, first, end):
             nc.vector.quantize_mx(
@@ -222,13 +227,15 @@ def tile_predictor_pa_kernel(tc, x, W1, b1, out):
                 for j in EARLY:
                     mx_pass(acc[j][:], j, c, 0, COLS)
 
+        nc.vector.tensor_scalar(out=bias3[:], in0=bias[:], scalar1=3.0, scalar2=None, op0=ALU.mult)
+        nc.vector.tensor_scalar(out=bias_tile0[:], in0=bias[:], scalar1=count0[:, 0:1], scalar2=None, op0=ALU.mult)
+        nc.vector.tensor_scalar(out=bias_tile1[:], in0=bias[:], scalar1=count1[:, 0:1], scalar2=None, op0=ALU.mult)
+
         out_rows = out.rearrange("(i j) c -> i j c", j=TILES)
 
         def finish(sums, j, first, end):
             summed = stage.tile([P, end - first], F32, tag="summed", name="summed%d_%d" % (j, first))
-            nc.vector.scalar_tensor_tensor(
-                out=summed[:], in0=bias[:, first:end], scalar=count_of.get(j, 3.0), in1=sums, op0=ALU.mult, op1=ALU.add
-            )
+            nc.vector.tensor_tensor(out=summed[:], in0=sums, in1=bias_of.get(j, bias3)[:, first:end], op=ALU.add)
             result = keep.tile([P, end - first], F32, name="result%d_%d" % (j, first))
             nc.scalar.activation(out=result[:], in_=summed[:], func=ACT.Tanh)
             nc.sync.dma_start(out=out_rows[:, j, first:end], in_=result[:])

@@ -90,12 +90,12 @@ def tile_predictor_pa_kernel(tc, x, W1, b1, out):
             nc.vector.memset(grouped[:, TILES:SLOTS, :, :], 0.0)
             xg.append(grouped)
             xg_words.append(grouped[:].bitcast(F32))
-            xc.append(keep.tile([P, SLOTS, P], U32, name="xc%d" % g, align_bytes=64))
-            xs.append(keep.tile([P, SLOTS, P], U8, name="xs%d" % g, align_bytes=64))
+            xc.append(keep.tile([P, SLOTS, P], U32, name="xc%d" % g, align_bytes=256))
+            xs.append(keep.tile([P, SLOTS, P], U8, name="xs%d" % g, align_bytes=256))
         wc, ws, wg = [], [], {}
         for c in range(CHUNKS):
-            wc.append(keep.tile([P, COLS], U32, name="wc%d" % c, align_bytes=64))
-            ws.append(keep.tile([P, COLS], U8, name="ws%d" % c, align_bytes=64))
+            wc.append(keep.tile([P, COLS], U32, name="wc%d" % c, align_bytes=256))
+            ws.append(keep.tile([P, COLS], U8, name="ws%d" % c, align_bytes=256))
 
         bias3 = keep.tile([P, COLS], F32, name="bias3")
         bias_tile0 = keep.tile([P, COLS], F32, name="bias_tile0")

@@ -6,6 +6,7 @@ from concourse.masks import make_identity
 F32 = mybir.dt.float32
 BF16 = mybir.dt.bfloat16
 U32 = mybir.dt.uint32
+I32 = mybir.dt.int32
 U8 = mybir.dt.uint8
 FP8X4 = mybir.dt.float8_e4m3fn_x4
 ACT = mybir.ActivationFunctionType
@@ -86,12 +87,13 @@ def tile_predictor_pa_kernel(tc, x, W1, b1, out):
 
         xg, xg_words, xc, xs = [], [], [], []
         for g in range(SLABS):
-            grouped = keep.tile([P, SLOTS, P, 4], BF16, name="xg%d" % g, align_bytes=64)
-            nc.vector.memset(grouped[:, TILES:SLOTS, :, :], 0.0)
+            grouped = keep.tile([P, TILES, P, 4], BF16, name="xg%d" % g, align_bytes=64)
             xg.append(grouped)
             xg_words.append(grouped[:].bitcast(F32))
             xc.append(keep.tile([P, SLOTS, P], U32, name="xc%d" % g, align_bytes=256))
             xs.append(keep.tile([P, SLOTS, P], U8, name="xs%d" % g, align_bytes=256))
+            nc.vector.memset(xs[g][:].rearrange("p s r -> p (s r)").bitcast(U32), 0)
+            nc.vector.memset(xc[g][:, TILES:SLOTS, 0:1], 0)
         wc, ws, wg = [], [], {}
         for c in range(CHUNKS):
             wc.append(keep.tile([P, COLS], U32, name="wc%d" % c, align_bytes=256))
@@ -111,9 +113,10 @@ def tile_predictor_pa_kernel(tc, x, W1, b1, out):
 
         def move_by_one_column(g):
             nc.vector.tensor_copy(
-                out=xg[g][:, TILES:SLOTS, 1:P, :].rearrange("p s r t -> p s (r t)"),
-                in_=xg[g][:, MOVED : MOVED + 2, 0 : P - 1, :].rearrange("p s r t -> p s (r t)"),
+                out=xc[g][:, TILES:SLOTS, 1:P].bitcast(I32),
+                in_=xc[g][:, MOVED : MOVED + 2, 0 : P - 1].bitcast(I32),
             )
+            nc.vector.tensor_copy(out=xs[g][:, TILES:SLOTS, 1:P], in_=xs[g][:, MOVED : MOVED + 2, 0 : P - 1])
 
         def regroup(c):
             wg[c] = stage.tile([P, COLS, 4], BF16, tag="wg", name="wg%d" % c, align_bytes=64)
@@ -156,8 +159,6 @@ def tile_predictor_pa_kernel(tc, x, W1, b1, out):
             copy_out_pair(nc.scalar.copy, 3)
             if n == 0:
                 move_by_one_column(0)
-            if n == 1:
-                quantise_x(0, TILES, SLOTS)
             for g in range(1, SLABS if n < 2 else 2):
                 quantise_x(g, j0, j0 + 2)
 
@@ -218,11 +219,8 @@ def tile_predictor_pa_kernel(tc, x, W1, b1, out):
                 else:
                     move_by_one_column(g)
             quantise_chunk(c)
-            if g < SLABS:
-                if c % 2 == 1:
-                    quantise_x(g, TILES, SLOTS)
-                elif g >= 2:
-                    quantise_x(g, 2, 4)
+            if g < SLABS and c % 2 == 0 and g >= 2:
+                quantise_x(g, 2, 4)
             if c < CHUNK_BY_CHUNK:
                 for j in EARLY:
                     mx_pass(acc[j][:], j, c, 0, COLS)

@@ -45,6 +45,14 @@ def tile_predictor_pa_kernel(tc, x, W1, b1, out):
         psum = ctx.enter_context(tc.psum_pool(name="psum", bufs=1))
         ctx.enter_context(tc.manual_schedule())
 
+        xc, xs, ws = [], [], []
+        for g in range(SLABS):
+            xs.append(keep.tile([P, SLOTS, P], U8, name="xs%d" % g, align_bytes=256))
+        for c in range(CHUNKS):
+            ws.append(keep.tile([P, COLS], U8, name="ws%d" % c, align_bytes=256))
+        for g in range(SLABS):
+            xc.append(keep.tile([P, SLOTS, P], U32, name="xc%d" % g, align_bytes=256))
+
         x_rows = x.rearrange("(i j) k -> i j k", j=TILES)
         x_sb = {}
         w_raw = {}
@@ -85,19 +93,16 @@ def tile_predictor_pa_kernel(tc, x, W1, b1, out):
         nc.vector.memset(count1[0:1, :], 2.0)
 
 
-        xg, xg_words, xc, xs = [], [], [], []
+        xg, xg_words = [], []
         for g in range(SLABS):
             grouped = keep.tile([P, TILES, P, 4], BF16, name="xg%d" % g, align_bytes=64)
             xg.append(grouped)
             xg_words.append(grouped[:].bitcast(F32))
-            xc.append(keep.tile([P, SLOTS, P], U32, name="xc%d" % g, align_bytes=256))
-            xs.append(keep.tile([P, SLOTS, P], U8, name="xs%d" % g, align_bytes=256))
             nc.vector.memset(xs[g][:].rearrange("p s r -> p (s r)").bitcast(U32), 0)
             nc.vector.memset(xc[g][:, TILES:SLOTS, 0:1], 0)
-        wc, ws, wg = [], [], {}
+        wc, wg = [], {}
         for c in range(CHUNKS):
             wc.append(keep.tile([P, COLS], U32, name="wc%d" % c, align_bytes=256))
-            ws.append(keep.tile([P, COLS], U8, name="ws%d" % c, align_bytes=256))
 
         bias3 = keep.tile([P, COLS], F32, name="bias3")
         bias_tile0 = keep.tile([P, COLS], F32, name="bias_tile0")

@@ -27,7 +27,7 @@ EARLY = (6, 7, 0, 1, 2, 3, 4)
 LATE = 5
 LATE_GROUPS = ((7, 0, 256), (0, 256, 384), (1, 384, 512))
 CHUNK_BY_CHUNK = 9
-VECTOR_COLS = (336, 400, 224) + (192,) * 9
+VECTOR_COLS = (336, 336, 224) + (192,) * 9
 
 FLOPS = 2 * ROWS * K_DIM * COLS * TAPS
 
@@ -69,11 +69,7 @@ def tile_predictor_pa_kernel(tc, x, W1, b1, out):
             x_sb[j] = keep.tile([P, K_DIM], BF16, name="x_sb%d" % j)
             if j == 4:
                 load_chunk(0)
-            pieces = 2 if j == 6 else 1
-            width = K_DIM // pieces
-            for piece in range(pieces):
-                cols = slice(piece * width, (piece + 1) * width)
-                nc.sync.dma_start(out=x_sb[j][:, cols], in_=x_rows[:, j, cols])
+            nc.sync.dma_start(out=x_sb[j][:], in_=x_rows[:, j, :])
         for c in range(1, CHUNKS):
             load_chunk(c)
         bias = keep.tile([P, COLS], BF16, name="bias")
@@ -161,14 +157,16 @@ def tile_predictor_pa_kernel(tc, x, W1, b1, out):
             copy_out_pair(nc.vector.tensor_copy, 1)
             copy_out_pair(nc.scalar.copy, 2)
             quantise_x(0, j0, j0 + 2)
+            if n == 2:
+                regroup(0)
+                quantise_x(1, j0, j0 + 2)
+                quantise_chunk(0)
             copy_out_pair(nc.scalar.copy, 3)
             if n == 0:
                 move_by_one_column(0)
-            for g in range(1, SLABS if n < 2 else 2):
-                quantise_x(g, j0, j0 + 2)
-
-        regroup(0)
-        quantise_chunk(0)
+            if n < 2:
+                for g in range(1, SLABS):
+                    quantise_x(g, j0, j0 + 2)
 
         halves = {}
         for n, j in enumerate(SINGLES):

from contextlib import ExitStack

import concourse.mybir as mybir
from concourse.masks import make_identity

F32 = mybir.dt.float32
BF16 = mybir.dt.bfloat16
U32 = mybir.dt.uint32
I32 = mybir.dt.int32
U8 = mybir.dt.uint8
FP8X4 = mybir.dt.float8_e4m3fn_x4
ACT = mybir.ActivationFunctionType
ALU = mybir.AluOpType

P = 128
ROWS, K_DIM, COLS, TAPS = 1024, 2048, 512, 3
SLAB = 4 * P
SLABS = K_DIM // SLAB
CHUNKS = SLABS * TAPS
TILES = ROWS // P
SLOTS = TILES + 2
MOVED = 6

PAIRS = (6, 0, 2)
SINGLES = (4, 5)
EARLY = (6, 7, 0, 1, 2, 3, 4)
LATE = 5
LATE_GROUPS = ((7, 0, 256), (0, 256, 384), (1, 384, 512))
CHUNK_BY_CHUNK = 9
VECTOR_COLS = (336, 336, 224) + (192,) * 9

FLOPS = 2 * ROWS * K_DIM * COLS * TAPS


def slot_of(j, tap):
    source = j - tap
    return source if source >= 0 else source + SLOTS


def tile_predictor_pa_kernel(tc, x, W1, b1, out):
    nc = tc.nc
    with ExitStack() as ctx:
        keep = ctx.enter_context(tc.tile_pool(name="keep", bufs=1))
        stage = ctx.enter_context(tc.tile_pool(name="stage", bufs=3))
        psum = ctx.enter_context(tc.psum_pool(name="psum", bufs=1))
        ctx.enter_context(tc.manual_schedule())

        xc, xs, ws = [], [], []
        for g in range(SLABS):
            xs.append(keep.tile([P, SLOTS, P], U8, name="xs%d" % g, align_bytes=256))
        for c in range(CHUNKS):
            ws.append(keep.tile([P, COLS], U8, name="ws%d" % c, align_bytes=256))
        for g in range(SLABS):
            xc.append(keep.tile([P, SLOTS, P], U32, name="xc%d" % g, align_bytes=256))

        x_rows = x.rearrange("(i j) k -> i j k", j=TILES)
        x_sb = {}
        w_raw = {}

        def load_chunk(c):
            g, tap = divmod(c, TAPS)
            w_raw[c] = keep.tile([P, 4, COLS], BF16, name="w_raw%d" % c)
            nc.sync.dma_start(
                out=w_raw[c][:],
                in_=W1[tap, SLAB * g : SLAB * (g + 1), :].rearrange("(q t) c -> q t c", t=4),
            )

        for j in (6, 7, 0, 1, 2, 3, 4, 5):
            x_sb[j] = keep.tile([P, K_DIM], BF16, name="x_sb%d" % j)
            if j == 4:
                load_chunk(0)
            nc.sync.dma_start(out=x_sb[j][:], in_=x_rows[:, j, :])
        for c in range(1, CHUNKS):
            load_chunk(c)
        bias = keep.tile([P, COLS], BF16, name="bias")
        nc.sync.dma_start(out=bias[:], in_=b1.rearrange("o c -> (o c)").partition_broadcast(P))

        table_in = keep.tile([P, 1], F32, name="table_in")
        table_out = keep.tile([P, 1], F32, name="table_out")
        nc.vector.memset(table_in[:], 0.0)
        nc.scalar.activation(out=table_out[:], in_=table_in[:], func=ACT.Tanh)
        ident = keep.tile([P, P], F32, name="ident")
        make_identity(nc, ident[:])
        count0 = keep.tile([P, 1], F32, name="count0")
        count1 = keep.tile([P, 1], F32, name="count1")
        nc.vector.memset(count0[:], 3.0)
        nc.vector.memset(count0[0:1, :], 1.0)
        nc.vector.memset(count1[:], 3.0)
        nc.vector.memset(count1[0:1, :], 2.0)


        xg, xg_words = [], []
        for g in range(SLABS):
            grouped = keep.tile([P, TILES, P, 4], BF16, name="xg%d" % g, align_bytes=64)
            xg.append(grouped)
            xg_words.append(grouped[:].bitcast(F32))
            nc.vector.memset(xs[g][:].rearrange("p s r -> p (s r)").bitcast(U32), 0)
            nc.vector.memset(xc[g][:, TILES:SLOTS, 0:1], 0)
        wc, wg = [], {}
        for c in range(CHUNKS):
            wc.append(keep.tile([P, COLS], U32, name="wc%d" % c, align_bytes=256))

        bias3 = keep.tile([P, COLS], F32, name="bias3")
        bias_tile0 = keep.tile([P, COLS], F32, name="bias_tile0")
        bias_tile1 = keep.tile([P, COLS], F32, name="bias_tile1")
        bias_of = {0: bias_tile0, 1: bias_tile1}

        def quantise_x(g, first, end):
            nc.vector.quantize_mx(
                out=xc[g][:, first:end, :].rearrange("p s r -> p (s r)").bitcast(FP8X4),
                scales=xs[g][:, first:end, :].rearrange("p s r -> p (s r)"),
                in_=xg[g][:, first:end, :, :].rearrange("p s r t -> p (s r t)"),
            )

        def move_by_one_column(g):
            nc.vector.tensor_copy(
                out=xc[g][:, TILES:SLOTS, 1:P].bitcast(I32),
                in_=xc[g][:, MOVED : MOVED + 2, 0 : P - 1].bitcast(I32),
            )
            nc.vector.tensor_copy(out=xs[g][:, TILES:SLOTS, 1:P], in_=xs[g][:, MOVED : MOVED + 2, 0 : P - 1])

        def regroup(c):
            wg[c] = stage.tile([P, COLS, 4], BF16, tag="wg", name="wg%d" % c, align_bytes=64)
            for copy, first, end in (
                (nc.vector.tensor_copy, 0, VECTOR_COLS[c]),
                (nc.scalar.copy, VECTOR_COLS[c], COLS),
            ):
                copy(
                    out=wg[c][:, first:end, :].rearrange("p (c i) t -> p c t i", i=4),
                    in_=w_raw[c][:, :, first:end].rearrange("p t (c i) -> p c t i", i=4),
                )

        def quantise_chunk(c):
            nc.vector.quantize_mx(
                out=wc[c][:].bitcast(FP8X4),
                scales=ws[c][:],
                in_=wg[c][:].rearrange("p c t -> p (c t)"),
            )

        def transpose_tile(j, targets):
            words = x_sb[j][:].bitcast(F32)
            for g in range(SLABS):
                for u in range(2):
                    nc.tensor.transpose(targets[g][:, u, :], words[:, 256 * g + u : 256 * (g + 1) : 2], ident[:])

        for n, j0 in enumerate(PAIRS):
            banks = []
            for g in range(SLABS):
                banks.append(psum.tile([P, 2, 2, P], F32, tag="bank%d" % (4 * (n % 2) + g), name="pair%d_%d" % (j0, g)))
            transpose_tile(j0, [bank[:, 0, :, :] for bank in banks])
            transpose_tile(j0 + 1, [bank[:, 1, :, :] for bank in banks])

            def copy_out_pair(copy, g):
                copy(out=xg_words[g][:, j0 : j0 + 2, :, :], in_=banks[g][:].rearrange("p j u r -> p j r u"))

            copy_out_pair(nc.scalar.copy, 0)
            copy_out_pair(nc.vector.tensor_copy, 1)
            copy_out_pair(nc.scalar.copy, 2)
            quantise_x(0, j0, j0 + 2)
            if n == 2:
                regroup(0)
                quantise_x(1, j0, j0 + 2)
                quantise_chunk(0)
            copy_out_pair(nc.scalar.copy, 3)
            if n == 0:
                move_by_one_column(0)
            if n < 2:
                for g in range(1, SLABS):
                    quantise_x(g, j0, j0 + 2)

        halves = {}
        for n, j in enumerate(SINGLES):
            halves[j] = []
            for h in range(2):
                halves[j].append(psum.tile([P, 2, 2, P], F32, tag="bank%d" % (4 + 2 * n + h), name="single%d_%d" % (j, h)))

        def copy_out_single(copy, j, g):
            copy(out=xg_words[g][:, j, :, :], in_=halves[j][g // 2][:, g % 2, :, :].rearrange("p u r -> p r u"))

        transpose_tile(4, [halves[4][g // 2][:, g % 2, :, :] for g in range(SLABS)])
        copy_out_single(nc.scalar.copy, 4, 0)
        copy_out_single(nc.vector.tensor_copy, 4, 1)
        copy_out_single(nc.scalar.copy, 4, 2)
        copy_out_single(nc.vector.tensor_copy, 4, 3)
        quantise_x(0, 4, 5)
        transpose_tile(5, [halves[5][g // 2][:, g % 2, :, :] for g in range(SLABS)])
        copy_out_single(nc.scalar.copy, 5, 0)
        copy_out_single(nc.vector.tensor_copy, 5, 1)

        acc = {}
        for bank, j in enumerate(EARLY):
            acc[j] = psum.tile([P, COLS], F32, tag="bank%d" % bank, name="acc%d" % j)

        def mx_pass(target, j, c, first, end):
            g, tap = divmod(c, TAPS)
            s = slot_of(j, tap)
            nc.tensor.matmul_mx(
                out=target,
                lhsT=xc[g][:, s, :].bitcast(FP8X4),
                lhsT_scale=xs[g][:, s, :],
                rhs=wc[c][:, first:end].bitcast(FP8X4),
                rhs_scale=ws[c][:, first:end],
                start=(c == 0),
                stop=(c == CHUNKS - 1),
            )

        for j in EARLY:
            mx_pass(acc[j][:], j, 0, 0, COLS)
        regroup(1)
        quantise_chunk(1)
        quantise_x(0, 5, 6)
        for j in (7, 0, 1, 2, 3, 4, 6):
            mx_pass(acc[j][:], j, 1, 0, COLS)
        copy_out_single(nc.scalar.copy, 5, 2)
        copy_out_single(nc.vector.tensor_copy, 5, 3)
        for c in range(2, CHUNKS):
            regroup(c)
            g = c // 2
            if g < SLABS:
                if c % 2 == 0:
                    quantise_x(g, 4, 6)
                else:
                    move_by_one_column(g)
            quantise_chunk(c)
            if g < SLABS and c % 2 == 0 and g >= 2:
                quantise_x(g, 2, 4)
            if c < CHUNK_BY_CHUNK:
                for j in EARLY:
                    mx_pass(acc[j][:], j, c, 0, COLS)

        nc.vector.tensor_scalar(out=bias3[:], in0=bias[:], scalar1=3.0, scalar2=None, op0=ALU.mult)
        nc.vector.tensor_scalar(out=bias_tile0[:], in0=bias[:], scalar1=count0[:, 0:1], scalar2=None, op0=ALU.mult)
        nc.vector.tensor_scalar(out=bias_tile1[:], in0=bias[:], scalar1=count1[:, 0:1], scalar2=None, op0=ALU.mult)

        out_rows = out.rearrange("(i j) c -> i j c", j=TILES)

        def finish(sums, j, first, end):
            summed = stage.tile([P, end - first], F32, tag="summed", name="summed%d_%d" % (j, first))
            nc.vector.tensor_tensor(out=summed[:], in0=sums, in1=bias_of.get(j, bias3)[:, first:end], op=ALU.add)
            result = keep.tile([P, end - first], F32, name="result%d_%d" % (j, first))
            nc.scalar.activation(out=result[:], in_=summed[:], func=ACT.Tanh)
            nc.sync.dma_start(out=out_rows[:, j, first:end], in_=result[:])

        for j in EARLY:
            for c in range(CHUNK_BY_CHUNK, CHUNKS):
                mx_pass(acc[j][:], j, c, 0, COLS)
            finish(acc[j][:], j, 0, COLS)
        for bank, first, end in LATE_GROUPS:
            late = psum.tile([P, end - first], F32, tag="bank%d" % bank, name="late%d" % first)
            for c in range(CHUNKS):
                mx_pass(late[:], LATE, c, first, end)
            finish(late[:], LATE, first, end)
